import numpy as np
import ml_dtypes


def mxq(x, axis, fmt="e4m3"):
    dtype, down = {"e4m3": (ml_dtypes.float8_e4m3fn, 7), "e5m2": (ml_dtypes.float8_e5m2, 14)}[fmt]
    v = np.moveaxis(np.asarray(x, np.float32).astype(ml_dtypes.bfloat16).astype(np.float64), axis, -1)
    blocks = v.reshape(v.shape[:-1] + (-1, 32))
    amax = np.abs(blocks).max(-1, keepdims=True)
    byte = np.maximum(np.where(amax > 0, np.frexp(amax)[1] - 1 + 127, 0) - down, 1)
    scale = np.exp2(byte - 127.0)
    codes = (blocks / scale).astype(np.float32).astype(dtype).astype(np.float64)
    return np.moveaxis((codes * scale).reshape(v.shape), -1, axis)


WIDE = False


def mx_kscale(k):
    if not WIDE:
        return np.ones(k)
    levels = np.array([10, -10, 5, -5, 0])
    if k % 512:
        return np.exp2(np.random.permutation(np.resize(levels, k // 32))).repeat(32)
    a = np.empty((k // 512, 16))
    for p in range(k // 512):
        a[p, :8] = np.random.permutation(np.resize(levels, 8))
        for g in range(8):
            far = levels[np.abs(levels - a[p, g]) >= 10]
            a[p, g + 8] = far[np.random.randint(len(far))]
    return np.exp2(a.ravel()).repeat(32)


BF16 = ml_dtypes.bfloat16


def bf(x):
    return np.asarray(x, np.float32).astype(BF16)


def f64(x):
    return np.asarray(x).astype(np.float64)


B, K, N = 4096, 512, 1024


def setup_inputs():
    s = mx_kscale(K)
    return {"x": bf(np.random.standard_normal((B, K)) * s),
            "dft_real": bf(np.random.standard_normal((N, K)) / np.sqrt(K) / s[None, :]),
            "dft_imag": bf(np.random.standard_normal((N, K)) / np.sqrt(K) / s[None, :])}


def reference(x, dft_real, dft_imag):
    xq = mxq(f64(x), 1, "e4m3")
    rxs = xq @ mxq(f64(dft_real), 1, "e4m3").T
    ixs = xq @ mxq(f64(dft_imag), 1, "e4m3").T
    mag = np.log(rxs * rxs + ixs * ixs)
    return mag

@@ -1,0 +1,247 @@
+from contextlib import ExitStack
+
+import concourse.mybir as mybir
+from concourse.masks import make_identity
+
+F32 = mybir.dt.float32
+BF16 = mybir.dt.bfloat16
+U32 = mybir.dt.uint32
+U8 = mybir.dt.uint8
+FP8X4 = mybir.dt.float8_e4m3fn_x4
+FUNC = mybir.ActivationFunctionType
+ALU = mybir.AluOpType
+AXIS = mybir.AxisListType
+
+B, K, N = 4096, 512, 1024
+FLOPS = 2 * B * K * 2 * N
+P = 128
+HALF = 512
+GROUPS = 8
+ACT_I = (0, 1, 2, 4, 5, 11, 19, 27, 35, 39, 43, 51)
+LAG = {4: 6, 2: 4, 1: 4}
+X_T, X_X, X_Q = 0, 1, 3
+FIRST = (2, 3, 4)
+UNITS_PER_ADD = {0: 1, 1: 1, 14: 2, 15: 1}
+
+
+def tile_dft_t_kernel(tc, x, dft_real, dft_imag, out):
+    nc = tc.nc
+    with ExitStack() as ctx:
+        ctx.enter_context(tc.manual_schedule())
+        const = ctx.enter_context(tc.tile_pool(name="const", bufs=1))
+        raw = ctx.enter_context(tc.tile_pool(name="raw", bufs=1))
+        keep = ctx.enter_context(tc.tile_pool(name="keep", bufs=1))
+        stage = ctx.enter_context(tc.tile_pool(name="stage", bufs=3))
+        work = ctx.enter_context(tc.tile_pool(name="work", bufs=1))
+        psum = ctx.enter_context(tc.psum_pool(name="psum", bufs=1))
+
+        raws = {}
+
+        def load_x(g):
+            t = raw.tile([P, 4 * K], BF16, name="rawx%d" % g)
+            nc.sync.dma_start(
+                out=t[:].rearrange("p (t k) -> p t k", t=4),
+                in_=x[512 * g : 512 * (g + 1), :].rearrange("(p t) k -> p t k", t=4),
+            )
+            raws["x%d" % g] = t
+
+        def load_w(m, h):
+            src = (dft_real, dft_imag)[m]
+            t = raw.tile([P, 4 * K], BF16, name="raww%d%d" % (m, h))
+            nc.sync.dma_start(
+                out=t[:].rearrange("p (t k) -> p t k", t=4),
+                in_=src[HALF * h : HALF * (h + 1), :].rearrange("(t p) k -> p t k", p=P),
+            )
+            raws["w%d%d" % (m, h)] = t
+
+        load_x(0)
+        load_w(0, 0)
+        load_w(1, 0)
+        load_w(0, 1)
+        load_w(1, 1)
+        for g in range(1, GROUPS):
+            load_x(g)
+
+        ident = const.tile([P, P], F32, name="ident")
+        make_identity(nc, ident[:])
+        warm = const.tile([P, 1], F32, name="warm")
+        nc.vector.memset(warm[:], 1.0)
+        warm2 = const.tile([P, 1], F32, name="warm2")
+        nc.scalar.activation(out=warm2[:], in_=warm[:], func=FUNC.Ln)
+
+        tbanks = {}
+        grouped_of = {}
+        quantised = {}
+
+        def transposes(name, tags):
+            words = raws[name][:].bitcast(F32)
+            pair = []
+            for half in range(2):
+                bank = psum.tile([P, 2, 2, P], F32, tag=tags[half], name="t%d%s" % (half, name),
+                                 bufs=(2 if tags[half] == "tp" else 3))
+                for bb in range(2):
+                    for u in range(2):
+                        c0 = 256 * (2 * half + bb)
+                        nc.tensor.transpose(bank[:, bb, u, :], words[:, c0 + u : c0 + 256 : 2], ident[:])
+                pair.append(bank)
+            tbanks[name] = pair
+
+        def exits(name, engines):
+            grouped = stage.tile([P, 4 * HALF], BF16, tag="grouped", name="g" + name, align_bytes=64)
+            gw = grouped[:].bitcast(F32).rearrange("p (b c u) -> p b c u", b=4, u=2)
+            for half in range(2):
+                src_view = tbanks[name][half][:].rearrange("p b u c -> p b c u")
+                dst_view = gw[:, 2 * half : 2 * half + 2]
+                if engines[half] == "a":
+                    nc.scalar.copy(out=dst_view, in_=src_view)
+                else:
+                    nc.vector.tensor_copy(out=dst_view, in_=src_view)
+            grouped_of[name] = grouped
+
+        def quantise(name):
+            codes = keep.tile([P, HALF], U32, name="c" + name, align_bytes=64)
+            scales = keep.tile([P, HALF], U8, name="s" + name, align_bytes=64)
+            nc.vector.quantize_mx(out=codes[:].bitcast(FP8X4), scales=scales[:], in_=grouped_of[name][:])
+            quantised[name] = (codes, scales)
+
+        units = [(0, t, 0) for t in range(4)] + [(0, t, 1) for t in range(4)]
+        for g in range(1, GROUPS):
+            units += [(g, t, h) for t in range(4) for h in range(2)]
+        n_units = len(units)
+
+        at_t = {}
+        at_x = {}
+        at_q = {}
+        for g in range(1, GROUPS):
+            base = 8 * (g - 1)
+            steps = FIRST if g == 1 else (base + X_T, base + X_X, base + X_Q)
+            at_t[steps[0]] = g
+            at_x[steps[1]] = g
+            at_q[steps[2]] = g
+
+        banks = {}
+
+        def mm(s):
+            g, t, h = units[s]
+            xc, xs = quantised["x%d" % g]
+            pair = []
+            for m in range(2):
+                wc, ws = quantised["w%d%d" % (m, h)]
+                acc = psum.tile([P, HALF], F32, tag=("r", "i")[m], name="acc%d_%d" % (m, s), bufs=3)
+                nc.tensor.matmul_mx(
+                    out=acc[:],
+                    lhsT=xc[:, P * t : P * (t + 1)].bitcast(FP8X4),
+                    lhsT_scale=xs[:, P * t : P * (t + 1)],
+                    rhs=wc[:].bitcast(FP8X4),
+                    rhs_scale=ws[:],
+                    start=True,
+                    stop=True,
+                )
+                pair.append(acc)
+            banks[s] = pair
+
+        sq = {}
+        ready = {}
+        pending = []
+        served = [0]
+
+        def place(s):
+            g, t, h = units[s]
+            return 2 * g + t // 2, N * (t % 2) + HALF * h
+
+        def squares_scalar(s):
+            pk, c0 = place(s)
+            if pk not in sq:
+                a_t = work.tile([P, 2 * N], F32, tag="a", name="a%d" % pk, bufs=6)
+                b_t = work.tile([P, 2 * N], F32, tag="b", name="b%d" % pk, bufs=4)
+                sq[pk] = (a_t, b_t)
+                ready[pk] = []
+            a_t, b_t = sq[pk]
+            nc.scalar.activation(out=a_t[:, c0 : c0 + HALF], in_=banks[s][0][:], func=FUNC.Square)
+            if s in ACT_I:
+                nc.scalar.activation(out=b_t[:, c0 : c0 + HALF], in_=banks[s][1][:], func=FUNC.Square)
+
+        def squares_vector(s):
+            pk, c0 = place(s)
+            if s not in ACT_I:
+                nc.vector.tensor_reduce(
+                    out=sq[pk][1][:, c0 : c0 + HALF],
+                    in_=banks[s][1][:].unsqueeze(2).to_broadcast([P, HALF, 2]),
+                    axis=AXIS.X,
+                    op=ALU.mult,
+                )
+
+        def adds(s):
+            pk, c0 = place(s)
+            a_t, b_t = sq[pk]
+            ready[pk].append(c0)
+            per = UNITS_PER_ADD.get(pk, 4)
+            done = sorted(ready[pk])
+            if per == 1:
+                first = c0
+            elif per == 2:
+                first = N * (c0 // N)
+                if first not in done or first + HALF not in done:
+                    return
+            else:
+                first = 0
+                if len(done) < 4:
+                    return
+            width = per * HALF
+            cols = slice(first, first + width)
+            nc.gpsimd.tensor_tensor(out=a_t[:, cols], in0=a_t[:, cols], in1=b_t[:, cols], op=ALU.add)
+            for k in range(0, width, N):
+                pending.append((s + LAG[per] + k // HALF, pk, first + k, min(N, width - k)))
+
+        def finish(pk, c0, width):
+            a_t = sq[pk][0]
+            part = a_t[:, c0 : c0 + width]
+            nc.scalar.activation(out=part, in_=part, func=FUNC.Ln)
+            g = pk // 2
+            t = 2 * (pk % 2) + c0 // N
+            n0 = c0 % N
+            dst = out[512 * g : 512 * (g + 1), :].rearrange("(p t) n -> p t n", t=4)
+            nc.sync.dma_start(out=dst[:, t, n0 : n0 + width], in_=part)
+
+        def finish_due(s):
+            pending[served[0] :] = sorted(pending[served[0] :])
+            while served[0] < len(pending) and pending[served[0]][0] <= s:
+                item = pending[served[0]]
+                served[0] += 1
+                finish(item[1], item[2], item[3])
+
+        transposes("x0", ("tp", "tp"))
+        transposes("w00", ("i", "i"))
+        exits("x0", "va")
+        transposes("w10", ("tp", "tp"))
+        quantise("x0")
+        exits("w00", "av")
+        quantise("w00")
+        transposes("w01", ("i", "r"))
+        exits("w10", "av")
+        quantise("w10")
+        mm(0)
+        mm(1)
+        for s in range(n_units):
+            if s == 1:
+                transposes("w11", ("tp", "tp"))
+            if s == 2:
+                quantise("w11")
+            if s in at_t:
+                transposes("x%d" % at_t[s], ("tp", "tp"))
+            if s + 2 < n_units:
+                mm(s + 2)
+            squares_scalar(s)
+            if s in at_x:
+                exits("x%d" % at_x[s], "vv")
+            if s in at_q:
+                quantise("x%d" % at_q[s])
+            squares_vector(s)
+            adds(s)
+            if s == 0:
+                exits("w01", "av")
+            if s == 1:
+                quantise("w01")
+                exits("w11", "av")
+            finish_due(s)
+        finish_due(10 * n_units)

@@ -17,11 +17,16 @@ FLOPS = 2 * B * K * 2 * N
 P = 128
 HALF = 512
 GROUPS = 8
-ACT_I = (0, 1, 2, 4, 5, 11, 19, 27, 35, 39, 43, 51)
-LAG = {4: 6, 2: 4, 1: 4}
-X_T, X_X, X_Q = 0, 1, 3
-FIRST = (2, 3, 4)
-UNITS_PER_ADD = {0: 1, 1: 1, 14: 2, 15: 1}
+TENSOR_TILES = (4, 4, 4, 4, 4, 4, 4, 4)
+PATTERN = ["bbbbnnnn","bnbnbnbn","bnbnbnbn","bnbnbnbn","bnbnbnbn","bnbnbnbn","bnbnbnbn","bnbnbnbn"]
+MM_LEAD = 2
+GP_LAG = 1
+TADD_LAG = 2
+LN_LAG_B = 4
+LN_LAG_N = 4
+X_T, X_X, X_Q = 0, 1, 2
+SCALAR_I = (0, 8, 16, 24, 32, 40, 48, 56,)
+COPY_I = ()
 
 
 def tile_dft_t_kernel(tc, x, dft_real, dft_imag, out):
@@ -78,7 +83,7 @@ def tile_dft_t_kernel(tc, x, dft_real, dft_imag, out):
             pair = []
             for half in range(2):
                 bank = psum.tile([P, 2, 2, P], F32, tag=tags[half], name="t%d%s" % (half, name),
-                                 bufs=(2 if tags[half] == "tp" else 3))
+                                 bufs=(3 if tags[half] == "side" else 5))
                 for bb in range(2):
                     for u in range(2):
                         c0 = 256 * (2 * half + bb)
@@ -104,144 +109,189 @@ def tile_dft_t_kernel(tc, x, dft_real, dft_imag, out):
             nc.vector.quantize_mx(out=codes[:].bitcast(FP8X4), scales=scales[:], in_=grouped_of[name][:])
             quantised[name] = (codes, scales)
 
-        units = [(0, t, 0) for t in range(4)] + [(0, t, 1) for t in range(4)]
-        for g in range(1, GROUPS):
-            units += [(g, t, h) for t in range(4) for h in range(2)]
+        units = []
+        for g in range(GROUPS):
+            own = []
+            turned = []
+            for t in range(4):
+                own.append(("b", g, t, 1, 0, HALF))
+            e = TENSOR_TILES[g]
+            width = HALF - P * e
+            if width:
+                per = HALF // width
+                for t in range(0, 4, per):
+                    own.append(("b", g, t, per, P * (4 + e), width))
+            for j in range(e):
+                turned.append(("n", g, 4 + j))
+            count = len(own) + len(turned)
+            for k in range(count):
+                if PATTERN[g][k] == "b":
+                    units.append(own.pop(0))
+                else:
+                    units.append(turned.pop(0))
         n_units = len(units)
-
-        at_t = {}
-        at_x = {}
-        at_q = {}
-        for g in range(1, GROUPS):
-            base = 8 * (g - 1)
-            steps = FIRST if g == 1 else (base + X_T, base + X_X, base + X_Q)
-            at_t[steps[0]] = g
-            at_x[steps[1]] = g
-            at_q[steps[2]] = g
+        first_of = {}
+        for s in range(n_units):
+            if units[s][1] not in first_of:
+                first_of[units[s][1]] = s
 
         banks = {}
+        parts = {}
+        outs = {}
+
+        def mm_one(acc, lhs, rhs):
+            lc, ls, l0 = lhs
+            rc, rs, r0, n = rhs
+            nc.tensor.matmul_mx(
+                out=acc,
+                lhsT=lc[:, l0 : l0 + P].bitcast(FP8X4),
+                lhsT_scale=ls[:, l0 : l0 + P],
+                rhs=rc[:, r0 : r0 + n].bitcast(FP8X4),
+                rhs_scale=rs[:, r0 : r0 + n],
+                start=True,
+                stop=True,
+            )
 
         def mm(s):
-            g, t, h = units[s]
-            xc, xs = quantised["x%d" % g]
+            u = units[s]
+            xc, xs = quantised["x%d" % u[1]]
             pair = []
             for m in range(2):
-                wc, ws = quantised["w%d%d" % (m, h)]
-                acc = psum.tile([P, HALF], F32, tag=("r", "i")[m], name="acc%d_%d" % (m, s), bufs=3)
-                nc.tensor.matmul_mx(
-                    out=acc[:],
-                    lhsT=xc[:, P * t : P * (t + 1)].bitcast(FP8X4),
-                    lhsT_scale=xs[:, P * t : P * (t + 1)],
-                    rhs=wc[:].bitcast(FP8X4),
-                    rhs_scale=ws[:],
-                    start=True,
-                    stop=True,
-                )
+                acc = psum.tile([P, HALF], F32, tag="acc", name="acc%d_%d" % (m, s), bufs=5)
+                if u[0] == "n":
+                    wc, ws = quantised["w%d%d" % (m, u[2] // 4)]
+                    mm_one(acc[:], (wc, ws, P * (u[2] % 4)), (xc, xs, 0, HALF))
+                else:
+                    t, per, c0, width = u[2:]
+                    wc, ws = quantised["w%d%d" % (m, c0 // HALF)]
+                    for k in range(per):
+                        mm_one(acc[:, width * k : width * (k + 1)], (xc, xs, P * (t + k)), (wc, ws, c0 % HALF, width))
                 pair.append(acc)
             banks[s] = pair
 
-        sq = {}
-        ready = {}
-        pending = []
-        served = [0]
+        def out_view(s):
+            u = units[s]
+            o = outs[u[1]]
+            if u[0] == "n":
+                return o[:, :, P * u[2] : P * (u[2] + 1)]
+            t, per, c0, width = u[2:]
+            return o[:, t : t + per, c0 : c0 + width]
 
-        def place(s):
-            g, t, h = units[s]
-            return 2 * g + t // 2, N * (t % 2) + HALF * h
+        def split(s, ap):
+            u = units[s]
+            n = 4 if u[0] == "n" else u[3]
+            return ap.rearrange("p (t c) -> p t c", t=n)
 
         def squares_scalar(s):
-            pk, c0 = place(s)
-            if pk not in sq:
-                a_t = work.tile([P, 2 * N], F32, tag="a", name="a%d" % pk, bufs=6)
-                b_t = work.tile([P, 2 * N], F32, tag="b", name="b%d" % pk, bufs=4)
-                sq[pk] = (a_t, b_t)
-                ready[pk] = []
-            a_t, b_t = sq[pk]
-            nc.scalar.activation(out=a_t[:, c0 : c0 + HALF], in_=banks[s][0][:], func=FUNC.Square)
-            if s in ACT_I:
-                nc.scalar.activation(out=b_t[:, c0 : c0 + HALF], in_=banks[s][1][:], func=FUNC.Square)
+            u = units[s]
+            if u[1] not in outs:
+                outs[u[1]] = work.tile([P, 4, N], F32, tag="o", name="o%d" % u[1], bufs=3)
+            if u[0] == "n":
+                a_t = work.tile([P, HALF], F32, tag="na", name="na%d" % s, bufs=4)
+                b_t = work.tile([P, HALF], F32, tag="nb", name="nb%d" % s, bufs=4)
+                nc.scalar.activation(out=a_t[:], in_=banks[s][0][:], func=FUNC.Square)
+            else:
+                a_t = None
+                b_t = work.tile([P, HALF], F32, tag="b", name="b%d" % s, bufs=6)
+                nc.scalar.activation(out=out_view(s), in_=split(s, banks[s][0][:]), func=FUNC.Square)
+            parts[s] = (a_t, b_t)
+            if s in SCALAR_I:
+                nc.scalar.activation(out=b_t[:], in_=banks[s][1][:], func=FUNC.Square)
 
         def squares_vector(s):
-            pk, c0 = place(s)
-            if s not in ACT_I:
+            if s in SCALAR_I:
+                return
+            if s in COPY_I:
+                nc.vector.tensor_copy(out=parts[s][1][:], in_=banks[s][1][:])
+            else:
                 nc.vector.tensor_reduce(
-                    out=sq[pk][1][:, c0 : c0 + HALF],
+                    out=parts[s][1][:],
                     in_=banks[s][1][:].unsqueeze(2).to_broadcast([P, HALF, 2]),
                     axis=AXIS.X,
                     op=ALU.mult,
                 )
 
-        def adds(s):
-            pk, c0 = place(s)
-            a_t, b_t = sq[pk]
-            ready[pk].append(c0)
-            per = UNITS_PER_ADD.get(pk, 4)
-            done = sorted(ready[pk])
-            if per == 1:
-                first = c0
-            elif per == 2:
-                first = N * (c0 // N)
-                if first not in done or first + HALF not in done:
-                    return
-            else:
-                first = 0
-                if len(done) < 4:
-                    return
-            width = per * HALF
-            cols = slice(first, first + width)
-            nc.gpsimd.tensor_tensor(out=a_t[:, cols], in0=a_t[:, cols], in1=b_t[:, cols], op=ALU.add)
-            for k in range(0, width, N):
-                pending.append((s + LAG[per] + k // HALF, pk, first + k, min(N, width - k)))
+        def gp(s):
+            b_t = parts[s][1]
+            if s in COPY_I:
+                nc.gpsimd.tensor_tensor(out=b_t[:], in0=b_t[:], in1=b_t[:], op=ALU.mult)
+            if units[s][0] == "b":
+                o = out_view(s)
+                nc.gpsimd.tensor_tensor(out=o, in0=o, in1=split(s, b_t[:]), op=ALU.add)
 
-        def finish(pk, c0, width):
-            a_t = sq[pk][0]
-            part = a_t[:, c0 : c0 + width]
-            nc.scalar.activation(out=part, in_=part, func=FUNC.Ln)
-            g = pk // 2
-            t = 2 * (pk % 2) + c0 // N
-            n0 = c0 % N
+        sums = {}
+
+        def tensor_adds(s):
+            bank = psum.tile([P, 4, P], F32, tag="side", name="sum%d" % s, bufs=3)
+            for t in range(4):
+                for k in range(2):
+                    nc.tensor.matmul(
+                        out=bank[:, t, :],
+                        lhsT=parts[s][k][:, P * t : P * (t + 1)],
+                        rhs=ident[:],
+                        start=(k == 0),
+                        stop=(k == 1),
+                        is_transpose=True,
+                    )
+            sums[s] = bank
+
+        left = {}
+        for g in range(GROUPS):
+            left[g] = len([u for u in units if u[1] == g])
+
+        def finish(s):
+            u = units[s]
+            g = u[1]
+            o = out_view(s)
+            nc.scalar.activation(out=o, in_=(sums[s][:] if u[0] == "n" else o), func=FUNC.Ln)
+            left[g] -= 1
             dst = out[512 * g : 512 * (g + 1), :].rearrange("(p t) n -> p t n", t=4)
-            nc.sync.dma_start(out=dst[:, t, n0 : n0 + width], in_=part)
+            if u[0] == "b":
+                t, per, c0, width = u[2:]
+                nc.sync.dma_start(out=dst[:, t : t + per, c0 : c0 + width], in_=o)
+            else:
+                nc.sync.dma_start(out=dst[:, :, P * u[2] : P * (u[2] + 1)], in_=o)
 
-        def finish_due(s):
-            pending[served[0] :] = sorted(pending[served[0] :])
-            while served[0] < len(pending) and pending[served[0]][0] <= s:
-                item = pending[served[0]]
-                served[0] += 1
-                finish(item[1], item[2], item[3])
-
-        transposes("x0", ("tp", "tp"))
-        transposes("w00", ("i", "i"))
+        transposes("x0", ("side", "side"))
+        transposes("w00", ("acc", "acc"))
         exits("x0", "va")
-        transposes("w10", ("tp", "tp"))
+        transposes("w10", ("acc", "acc"))
         quantise("x0")
         exits("w00", "av")
         quantise("w00")
-        transposes("w01", ("i", "r"))
+        transposes("w01", ("side", "acc"))
         exits("w10", "av")
         quantise("w10")
-        mm(0)
-        mm(1)
-        for s in range(n_units):
-            if s == 1:
-                transposes("w11", ("tp", "tp"))
-            if s == 2:
-                quantise("w11")
-            if s in at_t:
-                transposes("x%d" % at_t[s], ("tp", "tp"))
-            if s + 2 < n_units:
-                mm(s + 2)
-            squares_scalar(s)
-            if s in at_x:
-                exits("x%d" % at_x[s], "vv")
-            if s in at_q:
-                quantise("x%d" % at_q[s])
-            squares_vector(s)
-            adds(s)
+        for s in range(MM_LEAD):
+            mm(s)
+        for s in range(n_units + 8):
+            for g in range(1, GROUPS):
+                if s == first_of[g - 1] + X_T:
+                    transposes("x%d" % g, ("side", "side"))
+            if s + MM_LEAD < n_units:
+                mm(s + MM_LEAD)
+            if 0 <= s - TADD_LAG < n_units and units[s - TADD_LAG][0] == "n":
+                tensor_adds(s - TADD_LAG)
+            if s < n_units:
+                squares_scalar(s)
+                squares_vector(s)
+            for g in range(1, GROUPS):
+                if s == first_of[g - 1] + X_X:
+                    exits("x%d" % g, "vv")
+                if s == first_of[g - 1] + X_Q:
+                    quantise("x%d" % g)
             if s == 0:
                 exits("w01", "av")
+                transposes("w11", ("side", "side"))
             if s == 1:
                 quantise("w01")
+            if s == 0:
                 exits("w11", "av")
-            finish_due(s)
-        finish_due(10 * n_units)
+            if s == 1:
+                quantise("w11")
+            if 0 <= s - GP_LAG < n_units:
+                gp(s - GP_LAG)
+            if 0 <= s - LN_LAG_B < n_units and units[s - LN_LAG_B][0] == "b":
+                finish(s - LN_LAG_B)
+            if 0 <= s - LN_LAG_N < n_units and units[s - LN_LAG_N][0] == "n":
+                finish(s - LN_LAG_N)

@@ -17,16 +17,13 @@ FLOPS = 2 * B * K * 2 * N
 P = 128
 HALF = 512
 GROUPS = 8
-TENSOR_TILES = (4, 4, 4, 4, 4, 4, 4, 4)
-PATTERN = ["bbbbnnnn","bnbnbnbn","bnbnbnbn","bnbnbnbn","bnbnbnbn","bnbnbnbn","bnbnbnbn","bnbnbnbn"]
+FIRST_ORDER, ORDER, LAST_ORDER = "nnnnbbbb", "bnbnbnbn", "bnbnbnbn"
 MM_LEAD = 2
 GP_LAG = 1
 TADD_LAG = 2
 LN_LAG_B = 4
 LN_LAG_N = 4
 X_T, X_X, X_Q = 0, 1, 2
-SCALAR_I = (0, 8, 16, 24, 32, 40, 48, 56,)
-COPY_I = ()
 
 
 def tile_dft_t_kernel(tc, x, dft_real, dft_imag, out):
@@ -41,31 +38,43 @@ def tile_dft_t_kernel(tc, x, dft_real, dft_imag, out):
         psum = ctx.enter_context(tc.psum_pool(name="psum", bufs=1))
 
         raws = {}
+        weights = (dft_real, dft_imag)
 
-        def load_x(g):
+        def load_x(g, pieces):
             t = raw.tile([P, 4 * K], BF16, name="rawx%d" % g)
-            nc.sync.dma_start(
-                out=t[:].rearrange("p (t k) -> p t k", t=4),
-                in_=x[512 * g : 512 * (g + 1), :].rearrange("(p t) k -> p t k", t=4),
-            )
+            view = t[:].rearrange("p (t k) -> p t k", t=4)
+            src = x[512 * g : 512 * (g + 1), :].rearrange("(p t) k -> p t k", t=4)
+            step = 4 // pieces
+            for c in range(0, 4, step):
+                nc.sync.dma_start(out=view[:, c : c + step], in_=src[:, c : c + step])
             raws["x%d" % g] = t
 
-        def load_w(m, h):
-            src = (dft_real, dft_imag)[m]
-            t = raw.tile([P, 4 * K], BF16, name="raww%d%d" % (m, h))
+        def load_w_tiles(j0, count):
+            t = raw.tile([P, 2, count, K], BF16, name="raww%d" % j0)
+            for m in range(2):
+                nc.sync.dma_start(
+                    out=t[:, m],
+                    in_=weights[m][P * j0 : P * (j0 + count), :].rearrange("(t p) k -> p t k", p=P),
+                )
+            for j in range(count):
+                raws["t%d" % (j0 + j)] = (t, j)
+
+        def load_w_half(m):
+            t = raw.tile([P, 4 * K], BF16, name="raww1%d" % m)
             nc.sync.dma_start(
                 out=t[:].rearrange("p (t k) -> p t k", t=4),
-                in_=src[HALF * h : HALF * (h + 1), :].rearrange("(t p) k -> p t k", p=P),
+                in_=weights[m][HALF:, :].rearrange("(t p) k -> p t k", p=P),
             )
-            raws["w%d%d" % (m, h)] = t
+            raws["w%d" % m] = t
 
-        load_x(0)
-        load_w(0, 0)
-        load_w(1, 0)
-        load_w(0, 1)
-        load_w(1, 1)
+        load_x(0, 2)
+        load_w_tiles(0, 1)
+        load_w_tiles(1, 1)
+        load_w_tiles(2, 2)
+        load_w_half(0)
+        load_w_half(1)
         for g in range(1, GROUPS):
-            load_x(g)
+            load_x(g, 1)
 
         ident = const.tile([P, P], F32, name="ident")
         make_identity(nc, ident[:])
@@ -77,13 +86,19 @@ def tile_dft_t_kernel(tc, x, dft_real, dft_imag, out):
         tbanks = {}
         grouped_of = {}
         quantised = {}
+        depth = {"side": 3, "acc": 5}
+
+        def copy_out(engine, dst, src):
+            if engine == "a":
+                nc.scalar.copy(out=dst, in_=src)
+            else:
+                nc.vector.tensor_copy(out=dst, in_=src)
 
         def transposes(name, tags):
             words = raws[name][:].bitcast(F32)
             pair = []
             for half in range(2):
-                bank = psum.tile([P, 2, 2, P], F32, tag=tags[half], name="t%d%s" % (half, name),
-                                 bufs=(3 if tags[half] == "side" else 5))
+                bank = psum.tile([P, 2, 2, P], F32, tag=tags[half], name="t%d%s" % (half, name), bufs=depth[tags[half]])
                 for bb in range(2):
                     for u in range(2):
                         c0 = 256 * (2 * half + bb)
@@ -95,12 +110,7 @@ def tile_dft_t_kernel(tc, x, dft_real, dft_imag, out):
             grouped = stage.tile([P, 4 * HALF], BF16, tag="grouped", name="g" + name, align_bytes=64)
             gw = grouped[:].bitcast(F32).rearrange("p (b c u) -> p b c u", b=4, u=2)
             for half in range(2):
-                src_view = tbanks[name][half][:].rearrange("p b u c -> p b c u")
-                dst_view = gw[:, 2 * half : 2 * half + 2]
-                if engines[half] == "a":
-                    nc.scalar.copy(out=dst_view, in_=src_view)
-                else:
-                    nc.vector.tensor_copy(out=dst_view, in_=src_view)
+                copy_out(engines[half], gw[:, 2 * half : 2 * half + 2], tbanks[name][half][:].rearrange("p b u c -> p b c u"))
             grouped_of[name] = grouped
 
         def quantise(name):
@@ -109,186 +119,175 @@ def tile_dft_t_kernel(tc, x, dft_real, dft_imag, out):
             nc.vector.quantize_mx(out=codes[:].bitcast(FP8X4), scales=scales[:], in_=grouped_of[name][:])
             quantised[name] = (codes, scales)
 
+        def tile_transposes(j, tag):
+            t, slot = raws["t%d" % j]
+            bank = psum.tile([P, 2, 2, P], F32, tag=tag, name="tt%d" % j, bufs=depth[tag])
+            for m in range(2):
+                words = t[:, m, slot].bitcast(F32)
+                for u in range(2):
+                    nc.tensor.transpose(bank[:, m, u, :], words[:, u::2], ident[:])
+            tbanks["t%d" % j] = bank
+
+        def tile_exit(j, engine):
+            grouped = stage.tile([P, 2 * HALF], BF16, tag="groupedt", name="gt%d" % j, align_bytes=64)
+            gw = grouped[:].bitcast(F32).rearrange("p (b c u) -> p b c u", b=2, u=2)
+            copy_out(engine, gw, tbanks["t%d" % j][:].rearrange("p b u c -> p b c u"))
+            grouped_of["t%d" % j] = grouped
+
+        def tile_quantise(j):
+            codes = keep.tile([P, 2 * P], U32, name="ct%d" % j, align_bytes=64)
+            scales = keep.tile([P, 2 * P], U8, name="st%d" % j, align_bytes=64)
+            nc.vector.quantize_mx(out=codes[:].bitcast(FP8X4), scales=scales[:], in_=grouped_of["t%d" % j][:])
+            quantised["t%d" % j] = (codes, scales)
+
         units = []
         for g in range(GROUPS):
-            own = []
-            turned = []
-            for t in range(4):
-                own.append(("b", g, t, 1, 0, HALF))
-            e = TENSOR_TILES[g]
-            width = HALF - P * e
-            if width:
-                per = HALF // width
-                for t in range(0, 4, per):
-                    own.append(("b", g, t, per, P * (4 + e), width))
-            for j in range(e):
-                turned.append(("n", g, 4 + j))
-            count = len(own) + len(turned)
-            for k in range(count):
-                if PATTERN[g][k] == "b":
-                    units.append(own.pop(0))
-                else:
-                    units.append(turned.pop(0))
+            order = FIRST_ORDER if g == 0 else LAST_ORDER if g == GROUPS - 1 else ORDER
+            for k in range(8):
+                units.append((order[k], g, order[:k].count(order[k])))
         n_units = len(units)
-        first_of = {}
-        for s in range(n_units):
-            if units[s][1] not in first_of:
-                first_of[units[s][1]] = s
 
         banks = {}
         parts = {}
         outs = {}
-
-        def mm_one(acc, lhs, rhs):
-            lc, ls, l0 = lhs
-            rc, rs, r0, n = rhs
-            nc.tensor.matmul_mx(
-                out=acc,
-                lhsT=lc[:, l0 : l0 + P].bitcast(FP8X4),
-                lhsT_scale=ls[:, l0 : l0 + P],
-                rhs=rc[:, r0 : r0 + n].bitcast(FP8X4),
-                rhs_scale=rs[:, r0 : r0 + n],
-                start=True,
-                stop=True,
-            )
+        sums = {}
 
         def mm(s):
-            u = units[s]
-            xc, xs = quantised["x%d" % u[1]]
+            kind, g, i = units[s]
+            xc, xs = quantised["x%d" % g]
             pair = []
             for m in range(2):
-                acc = psum.tile([P, HALF], F32, tag="acc", name="acc%d_%d" % (m, s), bufs=5)
-                if u[0] == "n":
-                    wc, ws = quantised["w%d%d" % (m, u[2] // 4)]
-                    mm_one(acc[:], (wc, ws, P * (u[2] % 4)), (xc, xs, 0, HALF))
+                acc = psum.tile([P, HALF], F32, tag="acc", name="acc%d_%d" % (m, s), bufs=depth["acc"])
+                if kind == "n":
+                    lc, ls = quantised["t%d" % i]
+                    l0 = P * m
+                    rc, rs = xc, xs
                 else:
-                    t, per, c0, width = u[2:]
-                    wc, ws = quantised["w%d%d" % (m, c0 // HALF)]
-                    for k in range(per):
-                        mm_one(acc[:, width * k : width * (k + 1)], (xc, xs, P * (t + k)), (wc, ws, c0 % HALF, width))
+                    lc, ls = xc, xs
+                    l0 = P * i
+                    rc, rs = quantised["w%d" % m]
+                nc.tensor.matmul_mx(
+                    out=acc[:],
+                    lhsT=lc[:, l0 : l0 + P].bitcast(FP8X4),
+                    lhsT_scale=ls[:, l0 : l0 + P],
+                    rhs=rc[:].bitcast(FP8X4),
+                    rhs_scale=rs[:],
+                    start=True,
+                    stop=True,
+                )
                 pair.append(acc)
             banks[s] = pair
 
-        def out_view(s):
-            u = units[s]
-            o = outs[u[1]]
-            if u[0] == "n":
-                return o[:, :, P * u[2] : P * (u[2] + 1)]
-            t, per, c0, width = u[2:]
-            return o[:, t : t + per, c0 : c0 + width]
+        def scalar_does_both(s):
+            return s % 8 == 0
 
-        def split(s, ap):
-            u = units[s]
-            n = 4 if u[0] == "n" else u[3]
-            return ap.rearrange("p (t c) -> p t c", t=n)
+        def gp_squares(s):
+            return False
 
         def squares_scalar(s):
-            u = units[s]
-            if u[1] not in outs:
-                outs[u[1]] = work.tile([P, 4, N], F32, tag="o", name="o%d" % u[1], bufs=3)
-            if u[0] == "n":
-                a_t = work.tile([P, HALF], F32, tag="na", name="na%d" % s, bufs=4)
-                b_t = work.tile([P, HALF], F32, tag="nb", name="nb%d" % s, bufs=4)
-                nc.scalar.activation(out=a_t[:], in_=banks[s][0][:], func=FUNC.Square)
+            kind, g, i = units[s]
+            if g not in outs:
+                outs[g] = work.tile([P, 4, N], F32, tag="o", name="o%d" % g, bufs=3)
+            if kind == "n":
+                a_t = work.tile([P, HALF], F32, tag="na", name="na%d" % s, bufs=4)[:]
+                b_t = work.tile([P, HALF], F32, tag="nb", name="nb%d" % s, bufs=4)[:]
             else:
-                a_t = None
-                b_t = work.tile([P, HALF], F32, tag="b", name="b%d" % s, bufs=6)
-                nc.scalar.activation(out=out_view(s), in_=split(s, banks[s][0][:]), func=FUNC.Square)
+                a_t = outs[g][:, i, HALF:]
+                b_t = work.tile([P, HALF], F32, tag="b", name="b%d" % s, bufs=6)[:]
+            nc.scalar.activation(out=a_t, in_=banks[s][0][:], func=FUNC.Square)
             parts[s] = (a_t, b_t)
-            if s in SCALAR_I:
-                nc.scalar.activation(out=b_t[:], in_=banks[s][1][:], func=FUNC.Square)
+            if scalar_does_both(s):
+                nc.scalar.activation(out=b_t, in_=banks[s][1][:], func=FUNC.Square)
 
         def squares_vector(s):
-            if s in SCALAR_I:
+            if scalar_does_both(s):
                 return
-            if s in COPY_I:
-                nc.vector.tensor_copy(out=parts[s][1][:], in_=banks[s][1][:])
+            if gp_squares(s):
+                nc.vector.tensor_copy(out=parts[s][1], in_=banks[s][1][:])
             else:
                 nc.vector.tensor_reduce(
-                    out=parts[s][1][:],
+                    out=parts[s][1],
                     in_=banks[s][1][:].unsqueeze(2).to_broadcast([P, HALF, 2]),
                     axis=AXIS.X,
                     op=ALU.mult,
                 )
 
         def gp(s):
-            b_t = parts[s][1]
-            if s in COPY_I:
-                nc.gpsimd.tensor_tensor(out=b_t[:], in0=b_t[:], in1=b_t[:], op=ALU.mult)
+            a_t, b_t = parts[s]
+            if gp_squares(s) and not scalar_does_both(s):
+                nc.gpsimd.tensor_tensor(out=b_t, in0=b_t, in1=b_t, op=ALU.mult)
             if units[s][0] == "b":
-                o = out_view(s)
-                nc.gpsimd.tensor_tensor(out=o, in0=o, in1=split(s, b_t[:]), op=ALU.add)
-
-        sums = {}
+                nc.gpsimd.tensor_tensor(out=a_t, in0=a_t, in1=b_t, op=ALU.add)
 
         def tensor_adds(s):
-            bank = psum.tile([P, 4, P], F32, tag="side", name="sum%d" % s, bufs=3)
-            for t in range(4):
-                for k in range(2):
+            bank = psum.tile([P, 4, P], F32, tag="side", name="sum%d" % s, bufs=depth["side"])
+            for k in range(2):
+                for t in range(4):
                     nc.tensor.matmul(
                         out=bank[:, t, :],
                         lhsT=parts[s][k][:, P * t : P * (t + 1)],
                         rhs=ident[:],
-                        start=(k == 0),
-                        stop=(k == 1),
+                        start=(k == 0 and t == 0),
+                        stop=(k == 1 and t == 3),
                         is_transpose=True,
                     )
             sums[s] = bank
 
-        left = {}
-        for g in range(GROUPS):
-            left[g] = len([u for u in units if u[1] == g])
-
         def finish(s):
-            u = units[s]
-            g = u[1]
-            o = out_view(s)
-            nc.scalar.activation(out=o, in_=(sums[s][:] if u[0] == "n" else o), func=FUNC.Ln)
-            left[g] -= 1
+            kind, g, i = units[s]
             dst = out[512 * g : 512 * (g + 1), :].rearrange("(p t) n -> p t n", t=4)
-            if u[0] == "b":
-                t, per, c0, width = u[2:]
-                nc.sync.dma_start(out=dst[:, t : t + per, c0 : c0 + width], in_=o)
+            if kind == "b":
+                o = outs[g][:, i, HALF:]
+                nc.scalar.activation(out=o, in_=o, func=FUNC.Ln)
+                nc.sync.dma_start(out=dst[:, i, HALF:], in_=o)
             else:
-                nc.sync.dma_start(out=dst[:, :, P * u[2] : P * (u[2] + 1)], in_=o)
+                o = outs[g][:, :, P * i : P * (i + 1)]
+                nc.scalar.activation(out=o, in_=sums[s][:], func=FUNC.Ln)
+                nc.sync.dma_start(out=dst[:, :, P * i : P * (i + 1)], in_=o)
 
         transposes("x0", ("side", "side"))
-        transposes("w00", ("acc", "acc"))
+        tile_transposes(0, "side")
         exits("x0", "va")
-        transposes("w10", ("acc", "acc"))
+        tile_transposes(1, "acc")
+        tile_exit(0, "a")
         quantise("x0")
-        exits("w00", "av")
-        quantise("w00")
-        transposes("w01", ("side", "acc"))
-        exits("w10", "av")
-        quantise("w10")
-        for s in range(MM_LEAD):
-            mm(s)
+        tile_quantise(0)
+        tile_exit(1, "v")
+        tile_transposes(2, "acc")
+        tile_transposes(3, "acc")
+        mm(0)
+        tile_quantise(1)
+        mm(1)
         for s in range(n_units + 8):
-            for g in range(1, GROUPS):
-                if s == first_of[g - 1] + X_T:
-                    transposes("x%d" % g, ("side", "side"))
-            if s + MM_LEAD < n_units:
+            if s == 0:
+                transposes("w0", ("side", "side"))
+            if s == 1:
+                transposes("w1", ("side", "side"))
+            if s < 8 * (GROUPS - 1) and s % 8 == X_T + (3 if s < 8 else 0):
+                transposes("x%d" % (s // 8 + 1), ("side", "side"))
+            if s < 2:
+                tile_exit(s + 2, "a" if s == 0 else "v")
+                tile_quantise(s + 2)
+            if MM_LEAD <= s + MM_LEAD < n_units and s + MM_LEAD >= 2:
                 mm(s + MM_LEAD)
             if 0 <= s - TADD_LAG < n_units and units[s - TADD_LAG][0] == "n":
                 tensor_adds(s - TADD_LAG)
             if s < n_units:
                 squares_scalar(s)
                 squares_vector(s)
-            for g in range(1, GROUPS):
-                if s == first_of[g - 1] + X_X:
-                    exits("x%d" % g, "vv")
-                if s == first_of[g - 1] + X_Q:
-                    quantise("x%d" % g)
             if s == 0:
-                exits("w01", "av")
-                transposes("w11", ("side", "side"))
+                exits("w0", "av")
             if s == 1:
-                quantise("w01")
-            if s == 0:
-                exits("w11", "av")
+                exits("w1", "av")
             if s == 1:
-                quantise("w11")
+                quantise("w0")
+            if s == 1:
+                quantise("w1")
+            if s < 8 * (GROUPS - 1):
+                if s % 8 == X_X + (3 if s < 8 else 0):
+                    exits("x%d" % (s // 8 + 1), "vv")
+                if s % 8 == X_Q + (3 if s < 8 else 0):
+                    quantise("x%d" % (s // 8 + 1))
             if 0 <= s - GP_LAG < n_units:
                 gp(s - GP_LAG)
             if 0 <= s - LN_LAG_B < n_units and units[s - LN_LAG_B][0] == "b":

@@ -17,7 +17,7 @@ FLOPS = 2 * B * K * 2 * N
 P = 128
 HALF = 512
 GROUPS = 8
-FIRST_ORDER, ORDER, LAST_ORDER = "nnnnbbbb", "bnbnbnbn", "bnbnbnbn"
+FIRST_ORDER, ORDER, LAST_ORDER = "nnnnbbbb", "bbcnbbcn", "bbcnbbcn"
 MM_LEAD = 2
 GP_LAG = 1
 TADD_LAG = 2
@@ -119,6 +119,23 @@ def tile_dft_t_kernel(tc, x, dft_real, dft_imag, out):
             nc.vector.quantize_mx(out=codes[:].bitcast(FP8X4), scales=scales[:], in_=grouped_of[name][:])
             quantised[name] = (codes, scales)
 
+        def pair_transposes(tags):
+            for m in range(2):
+                bank = psum.tile([P, 2, 2, P], F32, tag=tags[m], name="tp%d" % m, bufs=depth[tags[m]])
+                for j in range(2):
+                    t, slot = raws["t%d" % (2 + j)]
+                    words = t[:, m, slot].bitcast(F32)
+                    for u in range(2):
+                        nc.tensor.transpose(bank[:, j, u, :], words[:, u::2], ident[:])
+                tbanks["tp%d" % m] = bank
+
+        def pair_exits(engines):
+            grouped = stage.tile([P, 4 * HALF], BF16, tag="grouped", name="gtp", align_bytes=64)
+            gw = grouped[:].bitcast(F32).rearrange("p (b c u) -> p b c u", b=4, u=2)
+            for m in range(2):
+                copy_out(engines[m], gw[:, 2 * m : 2 * m + 2], tbanks["tp%d" % m][:].rearrange("p b u c -> p b c u"))
+            grouped_of["tp"] = grouped
+
         def tile_transposes(j, tag):
             t, slot = raws["t%d" % j]
             bank = psum.tile([P, 2, 2, P], F32, tag=tag, name="tt%d" % j, bufs=depth[tag])
@@ -152,29 +169,36 @@ def tile_dft_t_kernel(tc, x, dft_real, dft_imag, out):
         outs = {}
         sums = {}
 
+        def product(acc, lhs, rhs):
+            (lc, ls), l0 = lhs
+            (rc, rs), r0, n = rhs
+            nc.tensor.matmul_mx(
+                out=acc,
+                lhsT=lc[:, l0 : l0 + P].bitcast(FP8X4),
+                lhsT_scale=ls[:, l0 : l0 + P],
+                rhs=rc[:, r0 : r0 + n].bitcast(FP8X4),
+                rhs_scale=rs[:, r0 : r0 + n],
+                start=True,
+                stop=True,
+            )
+
         def mm(s):
             kind, g, i = units[s]
-            xc, xs = quantised["x%d" % g]
             pair = []
             for m in range(2):
                 acc = psum.tile([P, HALF], F32, tag="acc", name="acc%d_%d" % (m, s), bufs=depth["acc"])
                 if kind == "n":
-                    lc, ls = quantised["t%d" % i]
-                    l0 = P * m
-                    rc, rs = xc, xs
+                    lhs = (quantised["t%d" % i], P * m) if i < 2 else (quantised["tp"], 2 * P * m + P * (i - 2))
+                    product(acc[:], lhs, (quantised["x%d" % g], 0, HALF))
+                elif kind == "b":
+                    product(acc[:], (quantised["x%d" % g], P * i), (quantised["w%d" % m], 0, HALF))
                 else:
-                    lc, ls = xc, xs
-                    l0 = P * i
-                    rc, rs = quantised["w%d" % m]
-                nc.tensor.matmul_mx(
-                    out=acc[:],
-                    lhsT=lc[:, l0 : l0 + P].bitcast(FP8X4),
-                    lhsT_scale=ls[:, l0 : l0 + P],
-                    rhs=rc[:].bitcast(FP8X4),
-                    rhs_scale=rs[:],
-                    start=True,
-                    stop=True,
-                )
+                    for k in range(2):
+                        product(
+                            acc[:, 2 * P * k : 2 * P * (k + 1)],
+                            (quantised["x%d" % g], P * (2 * i + k)),
+                            (quantised["tp"], 2 * P * m, 2 * P),
+                        )
                 pair.append(acc)
             banks[s] = pair
 
@@ -184,6 +208,17 @@ def tile_dft_t_kernel(tc, x, dft_real, dft_imag, out):
         def gp_squares(s):
             return False
 
+        def out_view(s):
+            kind, g, i = units[s]
+            if kind == "n":
+                return outs[g][:, :, P * i : P * (i + 1)]
+            if kind == "b":
+                return outs[g][:, i, HALF:]
+            return outs[g][:, 2 * i : 2 * i + 2, 2 * P : HALF]
+
+        def split(s, ap):
+            return ap.rearrange("p (t c) -> p t c", t=2) if units[s][0] == "c" else ap
+
         def squares_scalar(s):
             kind, g, i = units[s]
             if g not in outs:
@@ -192,9 +227,9 @@ def tile_dft_t_kernel(tc, x, dft_real, dft_imag, out):
                 a_t = work.tile([P, HALF], F32, tag="na", name="na%d" % s, bufs=4)[:]
                 b_t = work.tile([P, HALF], F32, tag="nb", name="nb%d" % s, bufs=4)[:]
             else:
-                a_t = outs[g][:, i, HALF:]
+                a_t = out_view(s)
                 b_t = work.tile([P, HALF], F32, tag="b", name="b%d" % s, bufs=6)[:]
-            nc.scalar.activation(out=a_t, in_=banks[s][0][:], func=FUNC.Square)
+            nc.scalar.activation(out=a_t, in_=split(s, banks[s][0][:]), func=FUNC.Square)
             parts[s] = (a_t, b_t)
             if scalar_does_both(s):
                 nc.scalar.activation(out=b_t, in_=banks[s][1][:], func=FUNC.Square)
@@ -216,8 +251,8 @@ def tile_dft_t_kernel(tc, x, dft_real, dft_imag, out):
             a_t, b_t = parts[s]
             if gp_squares(s) and not scalar_does_both(s):
                 nc.gpsimd.tensor_tensor(out=b_t, in0=b_t, in1=b_t, op=ALU.mult)
-            if units[s][0] == "b":
-                nc.gpsimd.tensor_tensor(out=a_t, in0=a_t, in1=b_t, op=ALU.add)
+            if units[s][0] != "n":
+                nc.gpsimd.tensor_tensor(out=a_t, in0=a_t, in1=split(s, b_t), op=ALU.add)
 
         def tensor_adds(s):
             bank = psum.tile([P, 4, P], F32, tag="side", name="sum%d" % s, bufs=depth["side"])
@@ -235,15 +270,16 @@ def tile_dft_t_kernel(tc, x, dft_real, dft_imag, out):
 
         def finish(s):
             kind, g, i = units[s]
+            o = out_view(s)
+            nc.scalar.activation(out=o, in_=sums[s][:] if kind == "n" else o, func=FUNC.Ln)
             dst = out[512 * g : 512 * (g + 1), :].rearrange("(p t) n -> p t n", t=4)
-            if kind == "b":
-                o = outs[g][:, i, HALF:]
-                nc.scalar.activation(out=o, in_=o, func=FUNC.Ln)
-                nc.sync.dma_start(out=dst[:, i, HALF:], in_=o)
+            if kind == "n":
+                dst = dst[:, :, P * i : P * (i + 1)]
+            elif kind == "b":
+                dst = dst[:, i, HALF:]
             else:
-                o = outs[g][:, :, P * i : P * (i + 1)]
-                nc.scalar.activation(out=o, in_=sums[s][:], func=FUNC.Ln)
-                nc.sync.dma_start(out=dst[:, :, P * i : P * (i + 1)], in_=o)
+                dst = dst[:, 2 * i : 2 * i + 2, 2 * P : HALF]
+            nc.sync.dma_start(out=dst, in_=o)
 
         transposes("x0", ("side", "side"))
         tile_transposes(0, "side")
@@ -253,8 +289,7 @@ def tile_dft_t_kernel(tc, x, dft_real, dft_imag, out):
         quantise("x0")
         tile_quantise(0)
         tile_exit(1, "v")
-        tile_transposes(2, "acc")
-        tile_transposes(3, "acc")
+        pair_transposes(("acc", "acc"))
         mm(0)
         tile_quantise(1)
         mm(1)
@@ -265,9 +300,9 @@ def tile_dft_t_kernel(tc, x, dft_real, dft_imag, out):
                 transposes("w1", ("side", "side"))
             if s < 8 * (GROUPS - 1) and s % 8 == X_T + (3 if s < 8 else 0):
                 transposes("x%d" % (s // 8 + 1), ("side", "side"))
-            if s < 2:
-                tile_exit(s + 2, "a" if s == 0 else "v")
-                tile_quantise(s + 2)
+            if s == 0:
+                pair_exits("av")
+                quantise("tp")
             if MM_LEAD <= s + MM_LEAD < n_units and s + MM_LEAD >= 2:
                 mm(s + MM_LEAD)
             if 0 <= s - TADD_LAG < n_units and units[s - TADD_LAG][0] == "n":
@@ -290,7 +325,7 @@ def tile_dft_t_kernel(tc, x, dft_real, dft_imag, out):
                     quantise("x%d" % (s // 8 + 1))
             if 0 <= s - GP_LAG < n_units:
                 gp(s - GP_LAG)
-            if 0 <= s - LN_LAG_B < n_units and units[s - LN_LAG_B][0] == "b":
+            if 0 <= s - LN_LAG_B < n_units and units[s - LN_LAG_B][0] != "n":
                 finish(s - LN_LAG_B)
             if 0 <= s - LN_LAG_N < n_units and units[s - LN_LAG_N][0] == "n":
                 finish(s - LN_LAG_N)

@@ -17,7 +17,7 @@ FLOPS = 2 * B * K * 2 * N
 P = 128
 HALF = 512
 GROUPS = 8
-FIRST_ORDER, ORDER, LAST_ORDER = "nnnnbbbb", "bbcnbbcn", "bbcnbbcn"
+FIRST_ORDER, ORDER, LAST_ORDER = "nnccbbbb", "bbcnbbcn", "bbcnbbcn"
 MM_LEAD = 2
 GP_LAG = 1
 TADD_LAG = 2
@@ -119,22 +119,29 @@ def tile_dft_t_kernel(tc, x, dft_real, dft_imag, out):
             nc.vector.quantize_mx(out=codes[:].bitcast(FP8X4), scales=scales[:], in_=grouped_of[name][:])
             quantised[name] = (codes, scales)
 
-        def pair_transposes(tags):
-            for m in range(2):
-                bank = psum.tile([P, 2, 2, P], F32, tag=tags[m], name="tp%d" % m, bufs=depth[tags[m]])
-                for j in range(2):
-                    t, slot = raws["t%d" % (2 + j)]
-                    words = t[:, m, slot].bitcast(F32)
-                    for u in range(2):
-                        nc.tensor.transpose(bank[:, j, u, :], words[:, u::2], ident[:])
-                tbanks["tp%d" % m] = bank
+        def pair_transposes(m):
+            bank = psum.tile([P, 2, 2, P], F32, tag="side", name="tp%d" % m, bufs=depth["side"])
+            for j in range(2):
+                t, slot = raws["t%d" % (2 + j)]
+                words = t[:, m, slot].bitcast(F32)
+                for u in range(2):
+                    nc.tensor.transpose(bank[:, j, u, :], words[:, u::2], ident[:])
+            tbanks.setdefault("tp", []).append(bank)
 
-        def pair_exits(engines):
-            grouped = stage.tile([P, 4 * HALF], BF16, tag="grouped", name="gtp", align_bytes=64)
-            gw = grouped[:].bitcast(F32).rearrange("p (b c u) -> p b c u", b=4, u=2)
-            for m in range(2):
-                copy_out(engines[m], gw[:, 2 * m : 2 * m + 2], tbanks["tp%d" % m][:].rearrange("p b u c -> p b c u"))
-            grouped_of["tp"] = grouped
+        def quantise_part(name, first, width):
+            codes, scales = quantised[name]
+            cols = slice(first, first + width)
+            nc.vector.quantize_mx(
+                out=codes[:, cols].bitcast(FP8X4),
+                scales=scales[:, cols],
+                in_=grouped_of[name][:, 4 * first : 4 * (first + width)],
+            )
+
+        def bank_exit(name, half, engine):
+            if name not in grouped_of:
+                grouped_of[name] = stage.tile([P, 4 * HALF], BF16, tag="grouped", name="g" + name, align_bytes=64)
+            gw = grouped_of[name][:].bitcast(F32).rearrange("p (b c u) -> p b c u", b=4, u=2)
+            copy_out(engine, gw[:, 2 * half : 2 * half + 2], tbanks[name][half][:].rearrange("p b u c -> p b c u"))
 
         def tile_transposes(j, tag):
             t, slot = raws["t%d" % j]
@@ -203,7 +210,7 @@ def tile_dft_t_kernel(tc, x, dft_real, dft_imag, out):
             banks[s] = pair
 
         def scalar_does_both(s):
-            return s % 8 == 0
+            return s % 8 == 0 and s < 56
 
         def gp_squares(s):
             return False
@@ -281,48 +288,61 @@ def tile_dft_t_kernel(tc, x, dft_real, dft_imag, out):
                 dst = dst[:, 2 * i : 2 * i + 2, 2 * P : HALF]
             nc.sync.dma_start(out=dst, in_=o)
 
-        transposes("x0", ("side", "side"))
+        side = ("side", "side")
+        transposes("x0", side)
         tile_transposes(0, "side")
-        exits("x0", "va")
-        tile_transposes(1, "acc")
+        bank_exit("x0", 0, "v")
+        quantised["x0"] = (
+            keep.tile([P, HALF], U32, name="cx0", align_bytes=64),
+            keep.tile([P, HALF], U8, name="sx0", align_bytes=64),
+        )
+        quantise_part("x0", 0, HALF // 2)
+        bank_exit("x0", 1, "a")
+        quantise_part("x0", HALF // 2, HALF // 2)
         tile_exit(0, "a")
-        quantise("x0")
         tile_quantise(0)
-        tile_exit(1, "v")
-        pair_transposes(("acc", "acc"))
-        mm(0)
+        tile_transposes(1, "side")
+        tile_exit(1, "a")
         tile_quantise(1)
+        pair_transposes(0)
+        bank_exit("tp", 0, "a")
+        mm(0)
+        pair_transposes(1)
+        bank_exit("tp", 1, "v")
         mm(1)
         for s in range(n_units + 8):
             if s == 0:
-                transposes("w0", ("side", "side"))
-            if s == 1:
-                transposes("w1", ("side", "side"))
-            if s < 8 * (GROUPS - 1) and s % 8 == X_T + (3 if s < 8 else 0):
-                transposes("x%d" % (s // 8 + 1), ("side", "side"))
-            if s == 0:
-                pair_exits("av")
                 quantise("tp")
-            if MM_LEAD <= s + MM_LEAD < n_units and s + MM_LEAD >= 2:
-                mm(s + MM_LEAD)
+                transposes("w0", side)
+            if s == 1:
+                transposes("w1", side)
+            if s == 2:
+                transposes("x1", side)
+            if 8 <= s < 8 * (GROUPS - 1) and s % 8 == X_T:
+                transposes("x%d" % (s // 8 + 1), side)
             if 0 <= s - TADD_LAG < n_units and units[s - TADD_LAG][0] == "n":
                 tensor_adds(s - TADD_LAG)
             if s < n_units:
                 squares_scalar(s)
                 squares_vector(s)
-            if s == 0:
-                exits("w0", "av")
-            if s == 1:
-                exits("w1", "av")
+            if s < 2:
+                bank_exit("w%d" % s, 0, ("a", "a")[s])
+                bank_exit("w%d" % s, 1, ("a", "a")[s])
             if s == 1:
                 quantise("w0")
-            if s == 1:
+            if s == 2:
                 quantise("w1")
-            if s < 8 * (GROUPS - 1):
-                if s % 8 == X_X + (3 if s < 8 else 0):
+            if s == 3:
+                exits("x1", "vv")
+            if s == 4:
+                quantise("x1")
+            if 8 <= s < 8 * (GROUPS - 1):
+                if s % 8 == X_X:
                     exits("x%d" % (s // 8 + 1), "vv")
-                if s % 8 == X_Q + (3 if s < 8 else 0):
+                if s % 8 == X_Q:
                     quantise("x%d" % (s // 8 + 1))
+            if s + MM_LEAD < n_units:
+                mm(s + MM_LEAD)
             if 0 <= s - GP_LAG < n_units:
                 gp(s - GP_LAG)
             if 0 <= s - LN_LAG_B < n_units and units[s - LN_LAG_B][0] != "n":

@@ -17,7 +17,7 @@ FLOPS = 2 * B * K * 2 * N
 P = 128
 HALF = 512
 GROUPS = 8
-FIRST_ORDER, ORDER, LAST_ORDER = "nnccbbbb", "bbcnbbcn", "bbcnbbcn"
+FIRST_ORDER, ORDER, LAST_ORDER = "nnddbbbb", "bnbnbdbn", "bnbnbdbn"
 MM_LEAD = 2
 GP_LAG = 1
 TADD_LAG = 2
@@ -83,6 +83,16 @@ def tile_dft_t_kernel(tc, x, dft_real, dft_imag, out):
         warm2 = const.tile([P, 1], F32, name="warm2")
         nc.scalar.activation(out=warm2[:], in_=warm[:], func=FUNC.Ln)
 
+        zeros = const.tile([P, HALF], BF16, name="zeros")
+        nc.vector.memset(zeros[:], 0.0)
+        idle_bank = psum.tile([P, HALF], F32, tag="acc", name="idle", bufs=5)
+
+        def keep_warm(count):
+            for k in range(count):
+                nc.tensor.matmul(out=idle_bank[:], lhsT=zeros[:, :P], rhs=zeros[:], start=True, stop=True)
+
+        keep_warm(4)
+
         tbanks = {}
         grouped_of = {}
         quantised = {}
@@ -118,15 +128,6 @@ def tile_dft_t_kernel(tc, x, dft_real, dft_imag, out):
             scales = keep.tile([P, HALF], U8, name="s" + name, align_bytes=64)
             nc.vector.quantize_mx(out=codes[:].bitcast(FP8X4), scales=scales[:], in_=grouped_of[name][:])
             quantised[name] = (codes, scales)
-
-        def pair_transposes(m):
-            bank = psum.tile([P, 2, 2, P], F32, tag="side", name="tp%d" % m, bufs=depth["side"])
-            for j in range(2):
-                t, slot = raws["t%d" % (2 + j)]
-                words = t[:, m, slot].bitcast(F32)
-                for u in range(2):
-                    nc.tensor.transpose(bank[:, j, u, :], words[:, u::2], ident[:])
-            tbanks.setdefault("tp", []).append(bank)
 
         def quantise_part(name, first, width):
             codes, scales = quantised[name]
@@ -176,6 +177,10 @@ def tile_dft_t_kernel(tc, x, dft_real, dft_imag, out):
         outs = {}
         sums = {}
 
+        def tile_of(s):
+            kind, g, i = units[s]
+            return i if kind == "n" else 3 - i
+
         def product(acc, lhs, rhs):
             (lc, ls), l0 = lhs
             (rc, rs), r0, n = rhs
@@ -195,16 +200,15 @@ def tile_dft_t_kernel(tc, x, dft_real, dft_imag, out):
             for m in range(2):
                 acc = psum.tile([P, HALF], F32, tag="acc", name="acc%d_%d" % (m, s), bufs=depth["acc"])
                 if kind == "n":
-                    lhs = (quantised["t%d" % i], P * m) if i < 2 else (quantised["tp"], 2 * P * m + P * (i - 2))
-                    product(acc[:], lhs, (quantised["x%d" % g], 0, HALF))
+                    product(acc[:], (quantised["t%d" % tile_of(s)], P * m), (quantised["x%d" % g], 0, HALF))
                 elif kind == "b":
                     product(acc[:], (quantised["x%d" % g], P * i), (quantised["w%d" % m], 0, HALF))
                 else:
-                    for k in range(2):
+                    for t in range(4):
                         product(
-                            acc[:, 2 * P * k : 2 * P * (k + 1)],
-                            (quantised["x%d" % g], P * (2 * i + k)),
-                            (quantised["tp"], 2 * P * m, 2 * P),
+                            acc[:, P * t : P * (t + 1)],
+                            (quantised["x%d" % g], P * t),
+                            (quantised["t%d" % tile_of(s)], P * m, P),
                         )
                 pair.append(acc)
             banks[s] = pair
@@ -217,14 +221,12 @@ def tile_dft_t_kernel(tc, x, dft_real, dft_imag, out):
 
         def out_view(s):
             kind, g, i = units[s]
-            if kind == "n":
-                return outs[g][:, :, P * i : P * (i + 1)]
             if kind == "b":
                 return outs[g][:, i, HALF:]
-            return outs[g][:, 2 * i : 2 * i + 2, 2 * P : HALF]
+            return outs[g][:, :, P * tile_of(s) : P * (tile_of(s) + 1)]
 
         def split(s, ap):
-            return ap.rearrange("p (t c) -> p t c", t=2) if units[s][0] == "c" else ap
+            return ap.rearrange("p (t c) -> p t c", t=4) if units[s][0] == "d" else ap
 
         def squares_scalar(s):
             kind, g, i = units[s]
@@ -280,12 +282,7 @@ def tile_dft_t_kernel(tc, x, dft_real, dft_imag, out):
             o = out_view(s)
             nc.scalar.activation(out=o, in_=sums[s][:] if kind == "n" else o, func=FUNC.Ln)
             dst = out[512 * g : 512 * (g + 1), :].rearrange("(p t) n -> p t n", t=4)
-            if kind == "n":
-                dst = dst[:, :, P * i : P * (i + 1)]
-            elif kind == "b":
-                dst = dst[:, i, HALF:]
-            else:
-                dst = dst[:, 2 * i : 2 * i + 2, 2 * P : HALF]
+            dst = dst[:, i, HALF:] if kind == "b" else dst[:, :, P * tile_of(s) : P * (tile_of(s) + 1)]
             nc.sync.dma_start(out=dst, in_=o)
 
         side = ("side", "side")
@@ -304,15 +301,16 @@ def tile_dft_t_kernel(tc, x, dft_real, dft_imag, out):
         tile_transposes(1, "side")
         tile_exit(1, "a")
         tile_quantise(1)
-        pair_transposes(0)
-        bank_exit("tp", 0, "a")
+        tile_transposes(2, "side")
+        tile_exit(2, "a")
         mm(0)
-        pair_transposes(1)
-        bank_exit("tp", 1, "v")
+        tile_transposes(3, "side")
+        tile_exit(3, "v")
         mm(1)
         for s in range(n_units + 8):
             if s == 0:
-                quantise("tp")
+                tile_quantise(2)
+                tile_quantise(3)
                 transposes("w0", side)
             if s == 1:
                 transposes("w1", side)

@@ -17,7 +17,7 @@ FLOPS = 2 * B * K * 2 * N
 P = 128
 HALF = 512
 GROUPS = 8
-FIRST_ORDER, ORDER, LAST_ORDER = "nnddbbbb", "bnbnbdbn", "bnbnbdbn"
+FIRST_ORDER, ORDER, LAST_ORDER = "ndddbbbb", "bnbdnbbn", "bnbdnbbn"
 MM_LEAD = 2
 GP_LAG = 1
 TADD_LAG = 2
@@ -83,20 +83,10 @@ def tile_dft_t_kernel(tc, x, dft_real, dft_imag, out):
         warm2 = const.tile([P, 1], F32, name="warm2")
         nc.scalar.activation(out=warm2[:], in_=warm[:], func=FUNC.Ln)
 
-        zeros = const.tile([P, HALF], BF16, name="zeros")
-        nc.vector.memset(zeros[:], 0.0)
-        idle_bank = psum.tile([P, HALF], F32, tag="acc", name="idle", bufs=5)
-
-        def keep_warm(count):
-            for k in range(count):
-                nc.tensor.matmul(out=idle_bank[:], lhsT=zeros[:, :P], rhs=zeros[:], start=True, stop=True)
-
-        keep_warm(4)
-
         tbanks = {}
         grouped_of = {}
         quantised = {}
-        depth = {"side": 3, "acc": 5}
+        depth = {"side": 3, "r": 2, "i": 3}
 
         def copy_out(engine, dst, src):
             if engine == "a":
@@ -169,17 +159,13 @@ def tile_dft_t_kernel(tc, x, dft_real, dft_imag, out):
         for g in range(GROUPS):
             order = FIRST_ORDER if g == 0 else LAST_ORDER if g == GROUPS - 1 else ORDER
             for k in range(8):
-                units.append((order[k], g, order[:k].count(order[k])))
+                units.append((order[k], g, order[:k].count("b") if order[k] == "b" else k - order[:k].count("b")))
         n_units = len(units)
 
         banks = {}
         parts = {}
         outs = {}
         sums = {}
-
-        def tile_of(s):
-            kind, g, i = units[s]
-            return i if kind == "n" else 3 - i
 
         def product(acc, lhs, rhs):
             (lc, ls), l0 = lhs
@@ -198,9 +184,10 @@ def tile_dft_t_kernel(tc, x, dft_real, dft_imag, out):
             kind, g, i = units[s]
             pair = []
             for m in range(2):
-                acc = psum.tile([P, HALF], F32, tag="acc", name="acc%d_%d" % (m, s), bufs=depth["acc"])
+                tag = ("r", "i")[m]
+                acc = psum.tile([P, HALF], F32, tag=tag, name="%s%d" % (tag, s), bufs=depth[tag])
                 if kind == "n":
-                    product(acc[:], (quantised["t%d" % tile_of(s)], P * m), (quantised["x%d" % g], 0, HALF))
+                    product(acc[:], (quantised["t%d" % i], P * m), (quantised["x%d" % g], 0, HALF))
                 elif kind == "b":
                     product(acc[:], (quantised["x%d" % g], P * i), (quantised["w%d" % m], 0, HALF))
                 else:
@@ -208,7 +195,7 @@ def tile_dft_t_kernel(tc, x, dft_real, dft_imag, out):
                         product(
                             acc[:, P * t : P * (t + 1)],
                             (quantised["x%d" % g], P * t),
-                            (quantised["t%d" % tile_of(s)], P * m, P),
+                            (quantised["t%d" % i], P * m, P),
                         )
                 pair.append(acc)
             banks[s] = pair
@@ -223,7 +210,7 @@ def tile_dft_t_kernel(tc, x, dft_real, dft_imag, out):
             kind, g, i = units[s]
             if kind == "b":
                 return outs[g][:, i, HALF:]
-            return outs[g][:, :, P * tile_of(s) : P * (tile_of(s) + 1)]
+            return outs[g][:, :, P * i : P * (i + 1)]
 
         def split(s, ap):
             return ap.rearrange("p (t c) -> p t c", t=4) if units[s][0] == "d" else ap
@@ -282,7 +269,7 @@ def tile_dft_t_kernel(tc, x, dft_real, dft_imag, out):
             o = out_view(s)
             nc.scalar.activation(out=o, in_=sums[s][:] if kind == "n" else o, func=FUNC.Ln)
             dst = out[512 * g : 512 * (g + 1), :].rearrange("(p t) n -> p t n", t=4)
-            dst = dst[:, i, HALF:] if kind == "b" else dst[:, :, P * tile_of(s) : P * (tile_of(s) + 1)]
+            dst = dst[:, i, HALF:] if kind == "b" else dst[:, :, P * i : P * (i + 1)]
             nc.sync.dma_start(out=dst, in_=o)
 
         side = ("side", "side")
@@ -314,7 +301,7 @@ def tile_dft_t_kernel(tc, x, dft_real, dft_imag, out):
                 transposes("w0", side)
             if s == 1:
                 transposes("w1", side)
-            if s == 2:
+            if s == 3:
                 transposes("x1", side)
             if 8 <= s < 8 * (GROUPS - 1) and s % 8 == X_T:
                 transposes("x%d" % (s // 8 + 1), side)
@@ -330,9 +317,9 @@ def tile_dft_t_kernel(tc, x, dft_real, dft_imag, out):
                 quantise("w0")
             if s == 2:
                 quantise("w1")
-            if s == 3:
-                exits("x1", "vv")
             if s == 4:
+                exits("x1", "vv")
+            if s == 5:
                 quantise("x1")
             if 8 <= s < 8 * (GROUPS - 1):
                 if s % 8 == X_X:

@@ -269,8 +269,12 @@ def tile_dft_t_kernel(tc, x, dft_real, dft_imag, out):
             o = out_view(s)
             nc.scalar.activation(out=o, in_=sums[s][:] if kind == "n" else o, func=FUNC.Ln)
             dst = out[512 * g : 512 * (g + 1), :].rearrange("(p t) n -> p t n", t=4)
-            dst = dst[:, i, HALF:] if kind == "b" else dst[:, :, P * i : P * (i + 1)]
-            nc.sync.dma_start(out=dst, in_=o)
+            if kind == "b":
+                nc.sync.dma_start(out=dst[:, i, HALF:], in_=o)
+            elif g == GROUPS - 1:
+                nc.sync.dma_start(out=dst[:, :, P * i : P * (i + 1)], in_=o)
+            elif i == 3:
+                nc.sync.dma_start(out=dst[:, :, :HALF], in_=outs[g][:, :, :HALF])
 
         side = ("side", "side")
         transposes("x0", side)

from contextlib import ExitStack

import concourse.mybir as mybir
from concourse.masks import make_identity

F32 = mybir.dt.float32
BF16 = mybir.dt.bfloat16
U32 = mybir.dt.uint32
U8 = mybir.dt.uint8
FP8X4 = mybir.dt.float8_e4m3fn_x4
FUNC = mybir.ActivationFunctionType
ALU = mybir.AluOpType
AXIS = mybir.AxisListType

B, K, N = 4096, 512, 1024
FLOPS = 2 * B * K * 2 * N
P = 128
HALF = 512
GROUPS = 8
FIRST_ORDER, ORDER, LAST_ORDER = "ndddbbbb", "bnbdnbbn", "bnbdnbbn"
MM_LEAD = 2
GP_LAG = 1
TADD_LAG = 2
LN_LAG_B = 4
LN_LAG_N = 4
X_T, X_X, X_Q = 0, 1, 2


def tile_dft_t_kernel(tc, x, dft_real, dft_imag, out):
    nc = tc.nc
    with ExitStack() as ctx:
        ctx.enter_context(tc.manual_schedule())
        const = ctx.enter_context(tc.tile_pool(name="const", bufs=1))
        raw = ctx.enter_context(tc.tile_pool(name="raw", bufs=1))
        keep = ctx.enter_context(tc.tile_pool(name="keep", bufs=1))
        stage = ctx.enter_context(tc.tile_pool(name="stage", bufs=3))
        work = ctx.enter_context(tc.tile_pool(name="work", bufs=1))
        psum = ctx.enter_context(tc.psum_pool(name="psum", bufs=1))

        raws = {}
        weights = (dft_real, dft_imag)

        def load_x(g, pieces):
            t = raw.tile([P, 4 * K], BF16, name="rawx%d" % g)
            view = t[:].rearrange("p (t k) -> p t k", t=4)
            src = x[512 * g : 512 * (g + 1), :].rearrange("(p t) k -> p t k", t=4)
            step = 4 // pieces
            for c in range(0, 4, step):
                nc.sync.dma_start(out=view[:, c : c + step], in_=src[:, c : c + step])
            raws["x%d" % g] = t

        def load_w_tiles(j0, count):
            t = raw.tile([P, 2, count, K], BF16, name="raww%d" % j0)
            for m in range(2):
                nc.sync.dma_start(
                    out=t[:, m],
                    in_=weights[m][P * j0 : P * (j0 + count), :].rearrange("(t p) k -> p t k", p=P),
                )
            for j in range(count):
                raws["t%d" % (j0 + j)] = (t, j)

        def load_w_half(m):
            t = raw.tile([P, 4 * K], BF16, name="raww1%d" % m)
            nc.sync.dma_start(
                out=t[:].rearrange("p (t k) -> p t k", t=4),
                in_=weights[m][HALF:, :].rearrange("(t p) k -> p t k", p=P),
            )
            raws["w%d" % m] = t

        load_x(0, 2)
        load_w_tiles(0, 1)
        load_w_tiles(1, 1)
        load_w_tiles(2, 2)
        load_w_half(0)
        load_w_half(1)
        for g in range(1, GROUPS):
            load_x(g, 1)

        ident = const.tile([P, P], F32, name="ident")
        make_identity(nc, ident[:])
        warm = const.tile([P, 1], F32, name="warm")
        nc.vector.memset(warm[:], 1.0)
        warm2 = const.tile([P, 1], F32, name="warm2")
        nc.scalar.activation(out=warm2[:], in_=warm[:], func=FUNC.Ln)

        tbanks = {}
        grouped_of = {}
        quantised = {}
        depth = {"side": 3, "r": 2, "i": 3}

        def copy_out(engine, dst, src):
            if engine == "a":
                nc.scalar.copy(out=dst, in_=src)
            else:
                nc.vector.tensor_copy(out=dst, in_=src)

        def transposes(name, tags):
            words = raws[name][:].bitcast(F32)
            pair = []
            for half in range(2):
                bank = psum.tile([P, 2, 2, P], F32, tag=tags[half], name="t%d%s" % (half, name), bufs=depth[tags[half]])
                for bb in range(2):
                    for u in range(2):
                        c0 = 256 * (2 * half + bb)
                        nc.tensor.transpose(bank[:, bb, u, :], words[:, c0 + u : c0 + 256 : 2], ident[:])
                pair.append(bank)
            tbanks[name] = pair

        def exits(name, engines):
            grouped = stage.tile([P, 4 * HALF], BF16, tag="grouped", name="g" + name, align_bytes=64)
            gw = grouped[:].bitcast(F32).rearrange("p (b c u) -> p b c u", b=4, u=2)
            for half in range(2):
                copy_out(engines[half], gw[:, 2 * half : 2 * half + 2], tbanks[name][half][:].rearrange("p b u c -> p b c u"))
            grouped_of[name] = grouped

        def quantise(name):
            codes = keep.tile([P, HALF], U32, name="c" + name, align_bytes=64)
            scales = keep.tile([P, HALF], U8, name="s" + name, align_bytes=64)
            nc.vector.quantize_mx(out=codes[:].bitcast(FP8X4), scales=scales[:], in_=grouped_of[name][:])
            quantised[name] = (codes, scales)

        def quantise_part(name, first, width):
            codes, scales = quantised[name]
            cols = slice(first, first + width)
            nc.vector.quantize_mx(
                out=codes[:, cols].bitcast(FP8X4),
                scales=scales[:, cols],
                in_=grouped_of[name][:, 4 * first : 4 * (first + width)],
            )

        def bank_exit(name, half, engine):
            if name not in grouped_of:
                grouped_of[name] = stage.tile([P, 4 * HALF], BF16, tag="grouped", name="g" + name, align_bytes=64)
            gw = grouped_of[name][:].bitcast(F32).rearrange("p (b c u) -> p b c u", b=4, u=2)
            copy_out(engine, gw[:, 2 * half : 2 * half + 2], tbanks[name][half][:].rearrange("p b u c -> p b c u"))

        def tile_transposes(j, tag):
            t, slot = raws["t%d" % j]
            bank = psum.tile([P, 2, 2, P], F32, tag=tag, name="tt%d" % j, bufs=depth[tag])
            for m in range(2):
                words = t[:, m, slot].bitcast(F32)
                for u in range(2):
                    nc.tensor.transpose(bank[:, m, u, :], words[:, u::2], ident[:])
            tbanks["t%d" % j] = bank

        def tile_exit(j, engine):
            grouped = stage.tile([P, 2 * HALF], BF16, tag="groupedt", name="gt%d" % j, align_bytes=64)
            gw = grouped[:].bitcast(F32).rearrange("p (b c u) -> p b c u", b=2, u=2)
            copy_out(engine, gw, tbanks["t%d" % j][:].rearrange("p b u c -> p b c u"))
            grouped_of["t%d" % j] = grouped

        def tile_quantise(j):
            codes = keep.tile([P, 2 * P], U32, name="ct%d" % j, align_bytes=64)
            scales = keep.tile([P, 2 * P], U8, name="st%d" % j, align_bytes=64)
            nc.vector.quantize_mx(out=codes[:].bitcast(FP8X4), scales=scales[:], in_=grouped_of["t%d" % j][:])
            quantised["t%d" % j] = (codes, scales)

        units = []
        for g in range(GROUPS):
            order = FIRST_ORDER if g == 0 else LAST_ORDER if g == GROUPS - 1 else ORDER
            for k in range(8):
                units.append((order[k], g, order[:k].count("b") if order[k] == "b" else k - order[:k].count("b")))
        n_units = len(units)

        banks = {}
        parts = {}
        outs = {}
        sums = {}

        def product(acc, lhs, rhs):
            (lc, ls), l0 = lhs
            (rc, rs), r0, n = rhs
            nc.tensor.matmul_mx(
                out=acc,
                lhsT=lc[:, l0 : l0 + P].bitcast(FP8X4),
                lhsT_scale=ls[:, l0 : l0 + P],
                rhs=rc[:, r0 : r0 + n].bitcast(FP8X4),
                rhs_scale=rs[:, r0 : r0 + n],
                start=True,
                stop=True,
            )

        def mm(s):
            kind, g, i = units[s]
            pair = []
            for m in range(2):
                tag = ("r", "i")[m]
                acc = psum.tile([P, HALF], F32, tag=tag, name="%s%d" % (tag, s), bufs=depth[tag])
                if kind == "n":
                    product(acc[:], (quantised["t%d" % i], P * m), (quantised["x%d" % g], 0, HALF))
                elif kind == "b":
                    product(acc[:], (quantised["x%d" % g], P * i), (quantised["w%d" % m], 0, HALF))
                else:
                    for t in range(4):
                        product(
                            acc[:, P * t : P * (t + 1)],
                            (quantised["x%d" % g], P * t),
                            (quantised["t%d" % i], P * m, P),
                        )
                pair.append(acc)
            banks[s] = pair

        def scalar_does_both(s):
            return s % 8 == 0 and s < 56

        def gp_squares(s):
            return False

        def out_view(s):
            kind, g, i = units[s]
            if kind == "b":
                return outs[g][:, i, HALF:]
            return outs[g][:, :, P * i : P * (i + 1)]

        def split(s, ap):
            return ap.rearrange("p (t c) -> p t c", t=4) if units[s][0] == "d" else ap

        def squares_scalar(s):
            kind, g, i = units[s]
            if g not in outs:
                outs[g] = work.tile([P, 4, N], F32, tag="o", name="o%d" % g, bufs=3)
            if kind == "n":
                a_t = work.tile([P, HALF], F32, tag="na", name="na%d" % s, bufs=4)[:]
                b_t = work.tile([P, HALF], F32, tag="nb", name="nb%d" % s, bufs=4)[:]
            else:
                a_t = out_view(s)
                b_t = work.tile([P, HALF], F32, tag="b", name="b%d" % s, bufs=6)[:]
            nc.scalar.activation(out=a_t, in_=split(s, banks[s][0][:]), func=FUNC.Square)
            parts[s] = (a_t, b_t)
            if scalar_does_both(s):
                nc.scalar.activation(out=b_t, in_=banks[s][1][:], func=FUNC.Square)

        def squares_vector(s):
            if scalar_does_both(s):
                return
            if gp_squares(s):
                nc.vector.tensor_copy(out=parts[s][1], in_=banks[s][1][:])
            else:
                nc.vector.tensor_reduce(
                    out=parts[s][1],
                    in_=banks[s][1][:].unsqueeze(2).to_broadcast([P, HALF, 2]),
                    axis=AXIS.X,
                    op=ALU.mult,
                )

        def gp(s):
            a_t, b_t = parts[s]
            if gp_squares(s) and not scalar_does_both(s):
                nc.gpsimd.tensor_tensor(out=b_t, in0=b_t, in1=b_t, op=ALU.mult)
            if units[s][0] != "n":
                nc.gpsimd.tensor_tensor(out=a_t, in0=a_t, in1=split(s, b_t), op=ALU.add)

        def tensor_adds(s):
            bank = psum.tile([P, 4, P], F32, tag="side", name="sum%d" % s, bufs=depth["side"])
            for k in range(2):
                for t in range(4):
                    nc.tensor.matmul(
                        out=bank[:, t, :],
                        lhsT=parts[s][k][:, P * t : P * (t + 1)],
                        rhs=ident[:],
                        start=(k == 0 and t == 0),
                        stop=(k == 1 and t == 3),
                        is_transpose=True,
                    )
            sums[s] = bank

        def finish(s):
            kind, g, i = units[s]
            o = out_view(s)
            nc.scalar.activation(out=o, in_=sums[s][:] if kind == "n" else o, func=FUNC.Ln)
            dst = out[512 * g : 512 * (g + 1), :].rearrange("(p t) n -> p t n", t=4)
            if kind == "b":
                nc.sync.dma_start(out=dst[:, i, HALF:], in_=o)
            elif g == GROUPS - 1:
                nc.sync.dma_start(out=dst[:, :, P * i : P * (i + 1)], in_=o)
            elif i == 3:
                nc.sync.dma_start(out=dst[:, :, :HALF], in_=outs[g][:, :, :HALF])

        side = ("side", "side")
        transposes("x0", side)
        tile_transposes(0, "side")
        bank_exit("x0", 0, "v")
        quantised["x0"] = (
            keep.tile([P, HALF], U32, name="cx0", align_bytes=64),
            keep.tile([P, HALF], U8, name="sx0", align_bytes=64),
        )
        quantise_part("x0", 0, HALF // 2)
        bank_exit("x0", 1, "a")
        quantise_part("x0", HALF // 2, HALF // 2)
        tile_exit(0, "a")
        tile_quantise(0)
        tile_transposes(1, "side")
        tile_exit(1, "a")
        tile_quantise(1)
        tile_transposes(2, "side")
        tile_exit(2, "a")
        mm(0)
        tile_transposes(3, "side")
        tile_exit(3, "v")
        mm(1)
        for s in range(n_units + 8):
            if s == 0:
                tile_quantise(2)
                tile_quantise(3)
                transposes("w0", side)
            if s == 1:
                transposes("w1", side)
            if s == 3:
                transposes("x1", side)
            if 8 <= s < 8 * (GROUPS - 1) and s % 8 == X_T:
                transposes("x%d" % (s // 8 + 1), side)
            if 0 <= s - TADD_LAG < n_units and units[s - TADD_LAG][0] == "n":
                tensor_adds(s - TADD_LAG)
            if s < n_units:
                squares_scalar(s)
                squares_vector(s)
            if s < 2:
                bank_exit("w%d" % s, 0, ("a", "a")[s])
                bank_exit("w%d" % s, 1, ("a", "a")[s])
            if s == 1:
                quantise("w0")
            if s == 2:
                quantise("w1")
            if s == 4:
                exits("x1", "vv")
            if s == 5:
                quantise("x1")
            if 8 <= s < 8 * (GROUPS - 1):
                if s % 8 == X_X:
                    exits("x%d" % (s // 8 + 1), "vv")
                if s % 8 == X_Q:
                    quantise("x%d" % (s // 8 + 1))
            if s + MM_LEAD < n_units:
                mm(s + MM_LEAD)
            if 0 <= s - GP_LAG < n_units:
                gp(s - GP_LAG)
            if 0 <= s - LN_LAG_B < n_units and units[s - LN_LAG_B][0] != "n":
                finish(s - LN_LAG_B)
            if 0 <= s - LN_LAG_N < n_units and units[s - LN_LAG_N][0] == "n":
                finish(s - LN_LAG_N)
